import numpy as np
import ml_dtypes

BF16 = ml_dtypes.bfloat16


def bf(x):
    return np.asarray(x, np.float32).astype(BF16)


def f32(x):
    return np.asarray(x, np.float32)


def f64(x):
    return np.asarray(x).astype(np.float64)


def striped(idx):
    return np.tile(idx.reshape(-1, 16).T, (8, 1))


D, S, N, F, T, P = 128, 512, 128, 128, 4, 2


def setup_inputs():
    return {"table": bf(np.random.standard_normal((D, S))), "w": bf(np.random.uniform(-1.0, 1.0, (D, T * F)) / np.sqrt(T * D)), "b": f32(0.1 * np.random.standard_normal((F, 1))), "offs": striped(np.random.permutation(S)[:N])}


def reference(table, w, b, offs):
    idx = offs[:16].T.reshape(-1)
    y = f64(w).T @ f64(table)[:, idx]
    res = np.zeros((F, N)) + f64(b)
    for t in range(T):
        d = t - P
        lo, hi = max(0, -d), min(N, N - d)
        res[:, lo:hi] += y[t * F:(t + 1) * F, lo + d:hi + d]
    return res

@@ -1,0 +1,55 @@
+import concourse.mybir as mybir
+
+BF16, F32, U16 = mybir.dt.bfloat16, mybir.dt.float32, mybir.dt.uint16
+ADD = mybir.AluOpType.add
+
+FEATURES = 128
+WORDS = 512
+POSITIONS = 128
+FILTERS = 128
+TAPS = 4
+CENTRE = 2
+PIECE = 64
+MARGIN = TAPS - 1 - CENTRE
+PADDED = POSITIONS + TAPS
+
+FLOPS = 2 * FEATURES * TAPS * FILTERS * POSITIONS
+
+
+def tile_qa_cnn_kernel(tc, table, w, b, offs, out):
+    nc = tc.nc
+    with (
+        tc.tile_pool(name="held", bufs=1) as held,
+        tc.psum_pool(name="psum", bufs=1) as psum,
+    ):
+        offsets = held.tile([FEATURES, POSITIONS // 16], U16, name="offsets")
+        nc.sync.dma_start(offsets[:], offs)
+        words = held.tile([FEATURES, WORDS], BF16, name="words")
+        nc.sync.dma_start(words[:], table)
+        weights = held.tile([FEATURES, TAPS * FILTERS], BF16, name="weights")
+        nc.sync.dma_start(weights[:, 0:FILTERS], w[:, 0:FILTERS])
+        nc.sync.dma_start(weights[:, FILTERS:], w[:, FILTERS:])
+        bias = held.tile([FILTERS, 1], F32, name="bias")
+        nc.sync.dma_start(bias[:], b)
+
+        zeros = held.tile([FEATURES, PADDED], BF16, name="zeros")
+        nc.vector.memset(zeros[:], 0.0)
+        total = psum.tile([FILTERS, PADDED], F32, name="total")
+        nc.tensor.matmul(total[:], zeros[:, 0:FILTERS], zeros[:], start=True, stop=False)
+
+        pieces = [(t, i) for t in range(TAPS) for i in range(0, POSITIONS, PIECE)]
+        for t, i in pieces:
+            column = i + CENTRE - t + MARGIN
+            nc.tensor.matmul(
+                total[:, column : column + PIECE],
+                weights[:, t * FILTERS : (t + 1) * FILTERS],
+                words[:].indirect(offsets[:, i // 16 : (i + PIECE) // 16]),
+                start=False,
+                stop=(t, i) == pieces[-1],
+            )
+
+        result = held.tile([FILTERS, POSITIONS], F32, name="result")
+        nc.vector.tensor_scalar(
+            result[:], total[:, MARGIN : MARGIN + POSITIONS], bias[:, 0:1], None, ADD
+        )
+        nc.sync.dma_start(out, result[:])

@@ -23,9 +23,9 @@ def tile_qa_cnn_kernel(tc, table, w, b, offs, out):
         tc.psum_pool(name="psum", bufs=1) as psum,
     ):
         offsets = held.tile([FEATURES, POSITIONS // 16], U16, name="offsets")
-        nc.sync.dma_start(offsets[:], offs)
         words = held.tile([FEATURES, WORDS], BF16, name="words")
         nc.sync.dma_start(words[:], table)
+        nc.sync.dma_start(offsets[:], offs)
         weights = held.tile([FEATURES, TAPS * FILTERS], BF16, name="weights")
         nc.sync.dma_start(weights[:, 0:FILTERS], w[:, 0:FILTERS])
         nc.sync.dma_start(weights[:, FILTERS:], w[:, FILTERS:])

@@ -9,7 +9,7 @@ POSITIONS = 128
 FILTERS = 128
 TAPS = 4
 CENTRE = 2
-PIECE = 64
+HALF = POSITIONS // 2
 MARGIN = TAPS - 1 - CENTRE
 PADDED = POSITIONS + TAPS
 
@@ -37,16 +37,18 @@ def tile_qa_cnn_kernel(tc, table, w, b, offs, out):
         total = psum.tile([FILTERS, PADDED], F32, name="total")
         nc.tensor.matmul(total[:], zeros[:, 0:FILTERS], zeros[:], start=True, stop=False)
 
-        pieces = [(t, i) for t in range(TAPS) for i in range(0, POSITIONS, PIECE)]
-        for t, i in pieces:
-            column = i + CENTRE - t + MARGIN
-            nc.tensor.matmul(
-                total[:, column : column + PIECE],
-                weights[:, t * FILTERS : (t + 1) * FILTERS],
-                words[:].indirect(offsets[:, i // 16 : (i + PIECE) // 16]),
-                start=False,
-                stop=(t, i) == pieces[-1],
-            )
+        for t in range(TAPS):
+            closing = t == TAPS - 1
+            piece = POSITIONS if closing else HALF
+            for i in range(0, POSITIONS, piece):
+                column = i + CENTRE - t + MARGIN
+                nc.tensor.matmul(
+                    total[:, column : column + piece],
+                    weights[:, t * FILTERS : (t + 1) * FILTERS],
+                    words[:].indirect(offsets[:, i // 16 : (i + piece) // 16]),
+                    start=False,
+                    stop=closing,
+                )
 
         result = held.tile([FILTERS, POSITIONS], F32, name="result")
         nc.vector.tensor_scalar(

@@ -27,31 +27,41 @@ def tile_qa_cnn_kernel(tc, table, w, b, offs, out):
         nc.sync.dma_start(words[:], table)
         nc.sync.dma_start(offsets[:], offs)
         weights = held.tile([FEATURES, TAPS * FILTERS], BF16, name="weights")
-        nc.sync.dma_start(weights[:, 0:FILTERS], w[:, 0:FILTERS])
-        nc.sync.dma_start(weights[:, FILTERS:], w[:, FILTERS:])
+        last = (TAPS - 1) * FILTERS
+        nc.sync.dma_start(weights[:, last:], w[:, last:])
+        nc.sync.dma_start(weights[:, 0:last], w[:, 0:last])
         bias = held.tile([FILTERS, 1], F32, name="bias")
         nc.sync.dma_start(bias[:], b)
 
         zeros = held.tile([FEATURES, PADDED], BF16, name="zeros")
         nc.vector.memset(zeros[:], 0.0)
-        total = psum.tile([FILTERS, PADDED], F32, name="total")
-        nc.tensor.matmul(total[:], zeros[:, 0:FILTERS], zeros[:], start=True, stop=False)
+        shifted = psum.tile([FILTERS, PADDED], F32, name="shifted")
+        nc.tensor.matmul(shifted[:], zeros[:, 0:FILTERS], zeros[:], start=True, stop=False)
+        centre = psum.tile([FILTERS, POSITIONS], F32, name="centre")
 
-        for t in range(TAPS):
-            closing = t == TAPS - 1
+        unshifted = held.tile([FILTERS, POSITIONS], F32, name="unshifted")
+        for t in (3, 2, 0, 1):
+            filters = weights[:, t * FILTERS : (t + 1) * FILTERS]
+            if t == CENTRE:
+                nc.tensor.matmul(
+                    centre[:], filters, words[:].indirect(offsets[:]), start=True, stop=True
+                )
+                nc.vector.tensor_scalar(unshifted[:], centre[:], bias[:, 0:1], None, ADD)
+                continue
+            closing = t == 1
             piece = POSITIONS if closing else HALF
             for i in range(0, POSITIONS, piece):
                 column = i + CENTRE - t + MARGIN
                 nc.tensor.matmul(
-                    total[:, column : column + piece],
-                    weights[:, t * FILTERS : (t + 1) * FILTERS],
+                    shifted[:, column : column + piece],
+                    filters,
                     words[:].indirect(offsets[:, i // 16 : (i + piece) // 16]),
                     start=False,
                     stop=closing,
                 )
 
         result = held.tile([FILTERS, POSITIONS], F32, name="result")
-        nc.vector.tensor_scalar(
-            result[:], total[:, MARGIN : MARGIN + POSITIONS], bias[:, 0:1], None, ADD
+        nc.vector.tensor_tensor(
+            result[:], shifted[:, MARGIN : MARGIN + POSITIONS], unshifted[:], ADD
         )
         nc.sync.dma_start(out, result[:])

import concourse.mybir as mybir

BF16, F32, U16 = mybir.dt.bfloat16, mybir.dt.float32, mybir.dt.uint16
ADD = mybir.AluOpType.add

FEATURES = 128
WORDS = 512
POSITIONS = 128
FILTERS = 128
TAPS = 4
CENTRE = 2
HALF = POSITIONS // 2
MARGIN = TAPS - 1 - CENTRE
PADDED = POSITIONS + TAPS

FLOPS = 2 * FEATURES * TAPS * FILTERS * POSITIONS


def tile_qa_cnn_kernel(tc, table, w, b, offs, out):
    nc = tc.nc
    with (
        tc.tile_pool(name="held", bufs=1) as held,
        tc.psum_pool(name="psum", bufs=1) as psum,
    ):
        offsets = held.tile([FEATURES, POSITIONS // 16], U16, name="offsets")
        words = held.tile([FEATURES, WORDS], BF16, name="words")
        nc.sync.dma_start(words[:], table)
        nc.sync.dma_start(offsets[:], offs)
        weights = held.tile([FEATURES, TAPS * FILTERS], BF16, name="weights")
        last = (TAPS - 1) * FILTERS
        nc.sync.dma_start(weights[:, last:], w[:, last:])
        nc.sync.dma_start(weights[:, 0:last], w[:, 0:last])
        bias = held.tile([FILTERS, 1], F32, name="bias")
        nc.sync.dma_start(bias[:], b)

        zeros = held.tile([FEATURES, PADDED], BF16, name="zeros")
        nc.vector.memset(zeros[:], 0.0)
        shifted = psum.tile([FILTERS, PADDED], F32, name="shifted")
        nc.tensor.matmul(shifted[:], zeros[:, 0:FILTERS], zeros[:], start=True, stop=False)
        centre = psum.tile([FILTERS, POSITIONS], F32, name="centre")

        unshifted = held.tile([FILTERS, POSITIONS], F32, name="unshifted")
        for t in (3, 2, 0, 1):
            filters = weights[:, t * FILTERS : (t + 1) * FILTERS]
            if t == CENTRE:
                nc.tensor.matmul(
                    centre[:], filters, words[:].indirect(offsets[:]), start=True, stop=True
                )
                nc.vector.tensor_scalar(unshifted[:], centre[:], bias[:, 0:1], None, ADD)
                continue
            closing = t == 1
            piece = POSITIONS if closing else HALF
            for i in range(0, POSITIONS, piece):
                column = i + CENTRE - t + MARGIN
                nc.tensor.matmul(
                    shifted[:, column : column + piece],
                    filters,
                    words[:].indirect(offsets[:, i // 16 : (i + piece) // 16]),
                    start=False,
                    stop=closing,
                )

        result = held.tile([FILTERS, POSITIONS], F32, name="result")
        nc.vector.tensor_tensor(
            result[:], shifted[:, MARGIN : MARGIN + POSITIONS], unshifted[:], ADD
        )
        nc.sync.dma_start(out, result[:])
